import numpy as np
import ml_dtypes


def mxq(x, axis, fmt="e4m3"):
    dtype, down = {"e4m3": (ml_dtypes.float8_e4m3fn, 7), "e5m2": (ml_dtypes.float8_e5m2, 14)}[fmt]
    v = np.moveaxis(np.asarray(x, np.float32).astype(ml_dtypes.bfloat16).astype(np.float64), axis, -1)
    blocks = v.reshape(v.shape[:-1] + (-1, 32))
    amax = np.abs(blocks).max(-1, keepdims=True)
    byte = np.maximum(np.where(amax > 0, np.frexp(amax)[1] - 1 + 127, 0) - down, 1)
    scale = np.exp2(byte - 127.0)
    codes = (blocks / scale).astype(np.float32).astype(dtype).astype(np.float64)
    return np.moveaxis((codes * scale).reshape(v.shape), -1, axis)


WIDE = False


def mx_kscale(k):
    if not WIDE:
        return np.ones(k)
    levels = np.array([10, -10, 5, -5, 0])
    a = np.random.permutation(np.resize(levels, k // 512 * 4)).reshape(k // 512, 4)
    idx = np.arange(k)
    return np.exp2(a[idx // 512, idx % 128 // 32])


BF16 = ml_dtypes.bfloat16


def bf(x):
    return np.asarray(x, np.float32).astype(BF16)


def f64(x):
    return np.asarray(x).astype(np.float64)


B, T, D, H = 2, 1024, 512, 2048
R = B * T
EPS = 1e-5


def sigmoid(v):
    return 1.0 / (1.0 + np.exp(-v))


def layer_norm(x, g, b):
    mu = x.mean(-1, keepdims=True)
    var = np.square(x - mu).mean(-1, keepdims=True)
    return (x - mu) / np.sqrt(var + EPS) * g + b


def setup_inputs():
    s, t = mx_kscale(D), mx_kscale(D)
    n = np.random.standard_normal
    return {"x": bf(n((B, T, D))), "yt": bf(n((B, T, D)) * 0.5 * t),
            "ln1_g": bf((1.0 + 0.2 * n(D)) * s), "ln1_b": bf(0.3 * n(D) * s),
            "Wq": bf(n((D, D)) * 1.5 / np.sqrt(D) / s[:, None]), "bq": bf(0.3 * n(D)),
            "Wo": bf(n((D, D)) * 2.5 / np.sqrt(D) / t[:, None]), "bo": bf(0.3 * n(D))}


def reference(x, yt, ln1_g, ln1_b, Wq, bq, Wo, bo):
    xr = f64(x).reshape(R, D)
    h = layer_norm(xr, f64(ln1_g), f64(ln1_b))
    q = (mxq(h, 1, "e4m3") @ mxq(f64(Wq), 0, "e4m3")) + f64(bq)
    y = sigmoid(q) * f64(yt).reshape(R, D)
    attn = (mxq(y, 1, "e4m3") @ mxq(f64(Wo), 0, "e4m3")) + f64(bo)
    return (attn + xr).reshape(B, T, D)

@@ -1,0 +1,283 @@
+import concourse.mybir as mybir
+from concourse.masks import make_identity
+
+F32 = mybir.dt.float32
+BF16 = mybir.dt.bfloat16
+U32 = mybir.dt.uint32
+U8 = mybir.dt.uint8
+FP8X4 = mybir.dt.float8_e4m3fn_x4
+ALU = mybir.AluOpType
+ACT = mybir.ActivationFunctionType
+
+P = 128
+PACK = 4
+D = P * PACK
+ROWS = 2048
+TILES = ROWS // P
+CHUNK_TILES = 2
+CHUNK_ROWS = CHUNK_TILES * P
+CHUNKS = TILES // CHUNK_TILES
+STATS_AHEAD = 5
+EPS = 1e-5
+
+FLOPS = 2 * 2 * ROWS * D * D
+
+
+def tile_attentionfreetransformerencoder_pb_kernel(tc, x, yt, ln1_g, ln1_b, Wq, bq, Wo, bo, out):
+    nc = tc.nc
+    x_view = x.flatten_outer_dims().rearrange("(p t) d -> p t d", t=TILES)
+    yt_view = yt.flatten_outer_dims().rearrange("(p t) d -> p t d", t=TILES)
+    out_view = out.flatten_outer_dims().rearrange("(p t) d -> p t d", t=TILES)
+
+    with (
+        tc.tile_pool(name="consts", bufs=1) as consts,
+        tc.tile_pool(name="resident", bufs=1) as resident,
+        tc.tile_pool(name="work", bufs=3) as work,
+        tc.psum_pool(name="psum", bufs=2) as psum,
+        tc.manual_schedule(),
+    ):
+        x_sb = [resident.tile([P, CHUNK_TILES, D], BF16, name="x%d" % c) for c in range(CHUNKS)]
+        yt_sb = [resident.tile([P, CHUNK_TILES, D], BF16, name="yt%d" % c) for c in range(CHUNKS)]
+        wq_raw = consts.tile([P, PACK, D], BF16, name="wq_raw")
+        wo_raw = consts.tile([P, PACK, D], BF16, name="wo_raw")
+        vec_rows = consts.tile([P, P], BF16, name="vec_rows")
+        bo_all = consts.tile([P, D], BF16, name="bo_all")
+
+        def load_chunk(dst, view, c):
+            nc.sync.dma_start(out=dst[c][:], in_=view[:, c * CHUNK_TILES : (c + 1) * CHUNK_TILES, :])
+
+        def load_weight(dst, w):
+            nc.sync.dma_start(out=dst[:], in_=w.rearrange("(j p) n -> p j n", p=P))
+
+        load_chunk(x_sb, x_view, 0)
+        nc.vector.memset(vec_rows[:], 0.0)
+        for i, vec in enumerate((ln1_g, ln1_b, bq)):
+            nc.sync.dma_start(
+                out=vec_rows[i * PACK : (i + 1) * PACK, :], in_=vec.rearrange("(j c) -> j c", c=P)
+            )
+        load_weight(wq_raw, Wq)
+        load_chunk(x_sb, x_view, 1)
+        load_chunk(x_sb, x_view, 2)
+        load_weight(wo_raw, Wo)
+        for c in range(3, CHUNKS):
+            load_chunk(x_sb, x_view, c)
+            load_chunk(yt_sb, yt_view, c - 3)
+        nc.sync.dma_start(out=bo_all[:], in_=bo.partition_broadcast(P))
+        for c in range(CHUNKS - 3, CHUNKS):
+            load_chunk(yt_sb, yt_view, c)
+
+        warm = consts.tile([P, 1], F32, name="warm")
+        nc.vector.memset(warm[:], 0.0)
+        warm_out = consts.tile([P, 1], F32, name="warm_out")
+        nc.scalar.activation(out=warm_out[:], in_=warm[:], func=ACT.Sigmoid)
+
+        ident_bf16 = consts.tile([P, P], BF16, name="ident_bf16")
+        make_identity(nc, ident_bf16[:])
+        ident_f32 = consts.tile([P, P], F32, name="ident_f32")
+        make_identity(nc, ident_f32[:])
+        neg_half = consts.tile([P, CHUNK_TILES], F32, name="neg_half")
+        nc.gpsimd.memset(neg_half[:], -0.5)
+
+        wq_grouped = consts.tile([P, D, PACK], BF16, name="wq_grouped", align_bytes=64)
+        wo_grouped = consts.tile([P, D, PACK], BF16, name="wo_grouped", align_bytes=64)
+        wq_codes = consts.tile([P, D], U32, name="wq_codes", align_bytes=64)
+        wq_scales = consts.tile([P, D], U8, name="wq_scales", align_bytes=64)
+        wo_codes = consts.tile([P, D], U32, name="wo_codes", align_bytes=64)
+        wo_scales = consts.tile([P, D], U8, name="wo_scales", align_bytes=64)
+        cols = consts.tile([P, 3 * PACK], F32, name="cols")
+        g_col = cols[:, 0:PACK]
+        b_col = cols[:, PACK : 2 * PACK]
+        bq_col = cols[:, 2 * PACK : 3 * PACK]
+
+        rstd, shift, xn, xnT, hT, h_grouped, h_codes, h_scales = {}, {}, {}, {}, {}, {}, {}, {}
+        qT, gate, ytT, y_grouped, y_codes, y_scales, o, res = {}, {}, {}, {}, {}, {}, {}, {}
+
+        def quantise(grouped, codes, scales):
+            nc.vector.quantize_mx(
+                out=codes[:].bitcast(FP8X4), scales=scales[:], in_=grouped[:].rearrange("p w j -> p (w j)")
+            )
+
+        def stats(c):
+            bn = work.tile([P, CHUNK_TILES, 6], F32, name="bn")
+            mean_var = work.tile([P, CHUNK_TILES, 2], F32, name="mean_var")
+            for i in range(CHUNK_TILES):
+                nc.vector.bn_stats(out=bn[:, i, :], in_=x_sb[c][:, i, :])
+                nc.vector.bn_aggr(out=mean_var[:, i, :], in_=bn[:, i, :])
+            var_eps = work.tile([P, CHUNK_TILES], F32, name="var_eps")
+            nc.gpsimd.tensor_scalar(
+                out=var_eps[:], in0=mean_var[:, :, 1], scalar1=EPS, scalar2=None, op0=ALU.add
+            )
+            rstd[c] = resident.tile([P, CHUNK_TILES], F32, name="rstd%d" % c)
+            nc.gpsimd.tensor_tensor(out=rstd[c][:], in0=var_eps[:], in1=neg_half[:], op=ALU.pow)
+            neg_mean = work.tile([P, CHUNK_TILES], F32, name="neg_mean")
+            nc.gpsimd.tensor_scalar(
+                out=neg_mean[:], in0=mean_var[:, :, 0], scalar1=-1.0, scalar2=None, op0=ALU.mult
+            )
+            shift[c] = resident.tile([P, CHUNK_TILES], F32, name="shift%d" % c)
+            nc.gpsimd.tensor_tensor(out=shift[c][:], in0=neg_mean[:], in1=rstd[c][:], op=ALU.mult)
+
+        def normalise(c):
+            xn[c] = work.tile([P, CHUNK_TILES, D], F32, name="xn")
+            for i in range(CHUNK_TILES):
+                nc.scalar.activation(
+                    out=xn[c][:, i, :],
+                    in_=x_sb[c][:, i, :],
+                    func=ACT.Identity,
+                    scale=rstd[c][:, i : i + 1],
+                    bias=shift[c][:, i : i + 1],
+                )
+
+        def transpose_x(c):
+            xnT[c] = []
+            for b in range(2):
+                bank = psum.tile([P, 2, CHUNK_ROWS], F32, name="xnT")
+                for jj in range(2):
+                    j = 2 * b + jj
+                    for i in range(CHUNK_TILES):
+                        nc.tensor.transpose(
+                            bank[:, jj, i * P : (i + 1) * P], xn[c][:, i, j * P : (j + 1) * P], ident_f32[:]
+                        )
+                xnT[c].append(bank)
+
+        def gain_shift(c):
+            hT[c] = work.tile([P, PACK, CHUNK_ROWS], BF16, name="hT")
+            for j in range(PACK):
+                nc.scalar.activation(
+                    out=hT[c][:, j, :],
+                    in_=xnT[c][j // 2][:, j % 2, :],
+                    func=ACT.Identity,
+                    scale=g_col[:, j : j + 1],
+                    bias=b_col[:, j : j + 1],
+                )
+
+        def group_h(c):
+            h_grouped[c] = work.tile([P, CHUNK_ROWS, PACK], BF16, name="h_grouped", align_bytes=64)
+            nc.vector.tensor_copy(out=h_grouped[c][:], in_=hT[c][:].rearrange("p j w -> p w j"))
+
+        def quantise_h(c):
+            h_codes[c] = work.tile([P, CHUNK_ROWS], U32, name="h_codes", align_bytes=64)
+            h_scales[c] = work.tile([P, CHUNK_ROWS], U8, name="h_scales", align_bytes=64)
+            quantise(h_grouped[c], h_codes[c], h_scales[c])
+
+        def q_matmuls(c):
+            qT[c] = []
+            for b in range(2):
+                bank = psum.tile([P, 2, CHUNK_ROWS], F32, name="qT")
+                for jj in range(2):
+                    j = 2 * b + jj
+                    nc.tensor.matmul_mx(
+                        out=bank[:, jj, :],
+                        lhsT=wq_codes[:, j * P : (j + 1) * P].bitcast(FP8X4),
+                        lhsT_scale=wq_scales[:, j * P : (j + 1) * P],
+                        rhs=h_codes[c][:].bitcast(FP8X4),
+                        rhs_scale=h_scales[c][:],
+                        start=True,
+                        stop=True,
+                    )
+                qT[c].append(bank)
+
+        def sigmoid(c):
+            gate[c] = work.tile([P, PACK, CHUNK_ROWS], F32, name="gate")
+            for j in range(PACK):
+                nc.scalar.activation(
+                    out=gate[c][:, j, :],
+                    in_=qT[c][j // 2][:, j % 2, :],
+                    func=ACT.Sigmoid,
+                    bias=bq_col[:, j : j + 1],
+                )
+
+        def transpose_yt(c):
+            ytT[c] = psum.tile([P, PACK, CHUNK_ROWS], BF16, name="ytT")
+            for j in range(PACK):
+                for i in range(CHUNK_TILES):
+                    nc.tensor.transpose(
+                        ytT[c][:, j, i * P : (i + 1) * P], yt_sb[c][:, i, j * P : (j + 1) * P], ident_bf16[:]
+                    )
+
+        def product(c):
+            y_grouped[c] = work.tile([P, CHUNK_ROWS, PACK], BF16, name="y_grouped", align_bytes=64)
+            nc.vector.tensor_tensor(
+                out=y_grouped[c][:],
+                in0=ytT[c][:].rearrange("p j w -> p w j"),
+                in1=gate[c][:].rearrange("p j w -> p w j"),
+                op=ALU.mult,
+            )
+
+        def quantise_y(c):
+            y_codes[c] = work.tile([P, CHUNK_ROWS], U32, name="y_codes", align_bytes=64)
+            y_scales[c] = work.tile([P, CHUNK_ROWS], U8, name="y_scales", align_bytes=64)
+            quantise(y_grouped[c], y_codes[c], y_scales[c])
+
+        def out_matmuls(c):
+            o[c] = []
+            for i in range(CHUNK_TILES):
+                bank = psum.tile([P, D], F32, name="o")
+                nc.tensor.matmul_mx(
+                    out=bank[:],
+                    lhsT=y_codes[c][:, i * P : (i + 1) * P].bitcast(FP8X4),
+                    lhsT_scale=y_scales[c][:, i * P : (i + 1) * P],
+                    rhs=wo_codes[:].bitcast(FP8X4),
+                    rhs_scale=wo_scales[:],
+                    start=True,
+                    stop=True,
+                )
+                o[c].append(bank)
+
+        def residual(c):
+            res[c] = resident.tile([P, CHUNK_TILES, D], F32, name="res%d" % c)
+            nc.gpsimd.tensor_tensor(
+                out=res[c][:],
+                in0=x_sb[c][:],
+                in1=bo_all[:].unsqueeze(1).to_broadcast([P, CHUNK_TILES, D]),
+                op=ALU.add,
+            )
+
+        def add_first(c):
+            nc.vector.tensor_tensor(out=res[c][:, 0, :], in0=o[c][0][:], in1=res[c][:, 0, :], op=ALU.add)
+
+        def add_second(c):
+            nc.vector.tensor_tensor(out=res[c][:, 1, :], in0=o[c][1][:], in1=res[c][:, 1, :], op=ALU.add)
+            nc.sync.dma_start(out=out_view[:, c * CHUNK_TILES : (c + 1) * CHUNK_TILES, :], in_=res[c][:])
+
+        def run(stage, c):
+            if 0 <= c < CHUNKS:
+                stage(c)
+
+        nc.scalar.copy(out=wq_grouped[:], in_=wq_raw[:].rearrange("p j n -> p n j"))
+        stats(0)
+        stats(1)
+        nc.gpsimd.tensor_scalar(
+            out=wo_grouped[:],
+            in0=wo_raw[:].rearrange("p j n -> p n j"),
+            scalar1=1.0,
+            scalar2=0.0,
+            op0=ALU.mult,
+            op1=ALU.add,
+        )
+        for c in range(2, STATS_AHEAD):
+            stats(c)
+        cols_ps = psum.tile([P, P], BF16, name="cols_ps", tag="ytT")
+        nc.tensor.transpose(cols_ps[:], vec_rows[:], ident_bf16[:])
+        nc.scalar.copy(out=cols[:], in_=cols_ps[:, 0 : 3 * PACK])
+        normalise(0)
+        normalise(1)
+        transpose_x(0)
+        quantise(wq_grouped, wq_codes, wq_scales)
+        quantise(wo_grouped, wo_codes, wo_scales)
+
+        for s in range(CHUNKS + 2):
+            run(gain_shift, s)
+            run(sigmoid, s - 1)
+            run(normalise, s + 2)
+            run(transpose_x, s + 1)
+            run(transpose_yt, s)
+            run(group_h, s)
+            run(add_first, s - 2)
+            run(quantise_h, s)
+            run(q_matmuls, s)
+            run(product, s - 1)
+            run(add_second, s - 2)
+            run(quantise_y, s - 1)
+            run(out_matmuls, s - 1)
+            run(stats, s + STATS_AHEAD)
+            run(residual, s)

@@ -225,7 +225,7 @@ def tile_attentionfreetransformerencoder_pb_kernel(tc, x, yt, ln1_g, ln1_b, Wq, 
 
         def residual(c):
             res[c] = resident.tile([P, CHUNK_TILES, D], F32, name="res%d" % c)
-            nc.gpsimd.tensor_tensor(
+            nc.vector.tensor_tensor(
                 out=res[c][:],
                 in0=x_sb[c][:],
                 in1=bo_all[:].unsqueeze(1).to_broadcast([P, CHUNK_TILES, D]),

@@ -152,7 +152,11 @@ def tile_attentionfreetransformerencoder_pb_kernel(tc, x, yt, ln1_g, ln1_b, Wq, 
 
         def group_h(c):
             h_grouped[c] = work.tile([P, CHUNK_ROWS, PACK], BF16, name="h_grouped", align_bytes=64)
-            nc.vector.tensor_copy(out=h_grouped[c][:], in_=hT[c][:].rearrange("p j w -> p w j"))
+            planes = hT[c][:].rearrange("p j w -> p w j")
+            if c % 2 == 0:
+                nc.vector.tensor_copy(out=h_grouped[c][:], in_=planes)
+            else:
+                nc.scalar.copy(out=h_grouped[c][:], in_=planes)
 
         def quantise_h(c):
             h_codes[c] = work.tile([P, CHUNK_ROWS], U32, name="h_codes", align_bytes=64)
@@ -244,17 +248,7 @@ def tile_attentionfreetransformerencoder_pb_kernel(tc, x, yt, ln1_g, ln1_b, Wq, 
                 stage(c)
 
         nc.scalar.copy(out=wq_grouped[:], in_=wq_raw[:].rearrange("p j n -> p n j"))
-        stats(0)
-        stats(1)
-        nc.gpsimd.tensor_scalar(
-            out=wo_grouped[:],
-            in0=wo_raw[:].rearrange("p j n -> p n j"),
-            scalar1=1.0,
-            scalar2=0.0,
-            op0=ALU.mult,
-            op1=ALU.add,
-        )
-        for c in range(2, STATS_AHEAD):
+        for c in range(STATS_AHEAD):
             stats(c)
         cols_ps = psum.tile([P, P], BF16, name="cols_ps", tag="ytT")
         nc.tensor.transpose(cols_ps[:], vec_rows[:], ident_bf16[:])
@@ -262,16 +256,17 @@ def tile_attentionfreetransformerencoder_pb_kernel(tc, x, yt, ln1_g, ln1_b, Wq, 
         normalise(0)
         normalise(1)
         transpose_x(0)
+        nc.vector.tensor_copy(out=wo_grouped[:], in_=wo_raw[:].rearrange("p j n -> p n j"))
         quantise(wq_grouped, wq_codes, wq_scales)
         quantise(wo_grouped, wo_codes, wo_scales)
 
         for s in range(CHUNKS + 2):
             run(gain_shift, s)
+            run(group_h, s)
             run(sigmoid, s - 1)
             run(normalise, s + 2)
             run(transpose_x, s + 1)
             run(transpose_yt, s)
-            run(group_h, s)
             run(add_first, s - 2)
             run(quantise_h, s)
             run(q_matmuls, s)

@@ -102,17 +102,18 @@ def tile_attentionfreetransformerencoder_pb_kernel(tc, x, yt, ln1_g, ln1_b, Wq, 
             mean_var = work.tile([P, CHUNK_TILES, 2], F32, name="mean_var")
             for i in range(CHUNK_TILES):
                 nc.vector.bn_stats(out=bn[:, i, :], in_=x_sb[c][:, i, :])
+            for i in range(CHUNK_TILES):
                 nc.vector.bn_aggr(out=mean_var[:, i, :], in_=bn[:, i, :])
             var_eps = work.tile([P, CHUNK_TILES], F32, name="var_eps")
             nc.gpsimd.tensor_scalar(
                 out=var_eps[:], in0=mean_var[:, :, 1], scalar1=EPS, scalar2=None, op0=ALU.add
             )
-            rstd[c] = resident.tile([P, CHUNK_TILES], F32, name="rstd%d" % c)
-            nc.gpsimd.tensor_tensor(out=rstd[c][:], in0=var_eps[:], in1=neg_half[:], op=ALU.pow)
             neg_mean = work.tile([P, CHUNK_TILES], F32, name="neg_mean")
             nc.gpsimd.tensor_scalar(
                 out=neg_mean[:], in0=mean_var[:, :, 0], scalar1=-1.0, scalar2=None, op0=ALU.mult
             )
+            rstd[c] = resident.tile([P, CHUNK_TILES], F32, name="rstd%d" % c)
+            nc.gpsimd.tensor_tensor(out=rstd[c][:], in0=var_eps[:], in1=neg_half[:], op=ALU.pow)
             shift[c] = resident.tile([P, CHUNK_TILES], F32, name="shift%d" % c)
             nc.gpsimd.tensor_tensor(out=shift[c][:], in0=neg_mean[:], in1=rstd[c][:], op=ALU.mult)
 
@@ -236,12 +237,15 @@ def tile_attentionfreetransformerencoder_pb_kernel(tc, x, yt, ln1_g, ln1_b, Wq, 
                 op=ALU.add,
             )
 
+        def add_store(c, i):
+            nc.vector.tensor_tensor(out=res[c][:, i, :], in0=o[c][i][:], in1=res[c][:, i, :], op=ALU.add)
+            nc.sync.dma_start(out=out_view[:, c * CHUNK_TILES + i, :], in_=res[c][:, i, :])
+
         def add_first(c):
-            nc.vector.tensor_tensor(out=res[c][:, 0, :], in0=o[c][0][:], in1=res[c][:, 0, :], op=ALU.add)
+            add_store(c, 0)
 
         def add_second(c):
-            nc.vector.tensor_tensor(out=res[c][:, 1, :], in0=o[c][1][:], in1=res[c][:, 1, :], op=ALU.add)
-            nc.sync.dma_start(out=out_view[:, c * CHUNK_TILES : (c + 1) * CHUNK_TILES, :], in_=res[c][:])
+            add_store(c, 1)
 
         def run(stage, c):
             if 0 <= c < CHUNKS:

@@ -18,6 +18,7 @@ CHUNK_TILES = 2
 CHUNK_ROWS = CHUNK_TILES * P
 CHUNKS = TILES // CHUNK_TILES
 STATS_AHEAD = 5
+RUN = 4
 EPS = 1e-5
 
 FLOPS = 2 * 2 * ROWS * D * D
@@ -92,6 +93,12 @@ def tile_attentionfreetransformerencoder_pb_kernel(tc, x, yt, ln1_g, ln1_b, Wq, 
         rstd, shift, xn, xnT, hT, h_grouped, h_codes, h_scales = {}, {}, {}, {}, {}, {}, {}, {}
         qT, gate, ytT, y_grouped, y_codes, y_scales, o, res = {}, {}, {}, {}, {}, {}, {}, {}
 
+        def regroup(copy, grouped, planes):
+            copy(
+                out=grouped[:].rearrange("p (c i) j -> p c j i", i=RUN),
+                in_=planes[:].rearrange("p j (c i) -> p c j i", i=RUN),
+            )
+
         def quantise(grouped, codes, scales):
             nc.vector.quantize_mx(
                 out=codes[:].bitcast(FP8X4), scales=scales[:], in_=grouped[:].rearrange("p w j -> p (w j)")
@@ -153,11 +160,7 @@ def tile_attentionfreetransformerencoder_pb_kernel(tc, x, yt, ln1_g, ln1_b, Wq, 
 
         def group_h(c):
             h_grouped[c] = work.tile([P, CHUNK_ROWS, PACK], BF16, name="h_grouped", align_bytes=64)
-            planes = hT[c][:].rearrange("p j w -> p w j")
-            if c % 2 == 0:
-                nc.vector.tensor_copy(out=h_grouped[c][:], in_=planes)
-            else:
-                nc.scalar.copy(out=h_grouped[c][:], in_=planes)
+            regroup(nc.vector.tensor_copy if c % 2 == 0 else nc.scalar.copy, h_grouped[c], hT[c])
 
         def quantise_h(c):
             h_codes[c] = work.tile([P, CHUNK_ROWS], U32, name="h_codes", align_bytes=64)
@@ -251,7 +254,7 @@ def tile_attentionfreetransformerencoder_pb_kernel(tc, x, yt, ln1_g, ln1_b, Wq, 
             if 0 <= c < CHUNKS:
                 stage(c)
 
-        nc.scalar.copy(out=wq_grouped[:], in_=wq_raw[:].rearrange("p j n -> p n j"))
+        regroup(nc.scalar.copy, wq_grouped, wq_raw)
         for c in range(STATS_AHEAD):
             stats(c)
         cols_ps = psum.tile([P, P], BF16, name="cols_ps", tag="ytT")
@@ -260,7 +263,7 @@ def tile_attentionfreetransformerencoder_pb_kernel(tc, x, yt, ln1_g, ln1_b, Wq, 
         normalise(0)
         normalise(1)
         transpose_x(0)
-        nc.vector.tensor_copy(out=wo_grouped[:], in_=wo_raw[:].rearrange("p j n -> p n j"))
+        regroup(nc.vector.tensor_copy, wo_grouped, wo_raw)
         quantise(wq_grouped, wq_codes, wq_scales)
         quantise(wo_grouped, wo_codes, wo_scales)
 

@@ -35,7 +35,6 @@ def tile_attentionfreetransformerencoder_pb_kernel(tc, x, yt, ln1_g, ln1_b, Wq, 
         tc.tile_pool(name="resident", bufs=1) as resident,
         tc.tile_pool(name="work", bufs=3) as work,
         tc.psum_pool(name="psum", bufs=2) as psum,
-        tc.manual_schedule(),
     ):
         x_sb = [resident.tile([P, CHUNK_TILES, D], BF16, name="x%d" % c) for c in range(CHUNKS)]
         yt_sb = [resident.tile([P, CHUNK_TILES, D], BF16, name="yt%d" % c) for c in range(CHUNKS)]

import concourse.mybir as mybir
from concourse.masks import make_identity

F32 = mybir.dt.float32
BF16 = mybir.dt.bfloat16
U32 = mybir.dt.uint32
U8 = mybir.dt.uint8
FP8X4 = mybir.dt.float8_e4m3fn_x4
ALU = mybir.AluOpType
ACT = mybir.ActivationFunctionType

P = 128
PACK = 4
D = P * PACK
ROWS = 2048
TILES = ROWS // P
CHUNK_TILES = 2
CHUNK_ROWS = CHUNK_TILES * P
CHUNKS = TILES // CHUNK_TILES
STATS_AHEAD = 5
RUN = 4
EPS = 1e-5

FLOPS = 2 * 2 * ROWS * D * D


def tile_attentionfreetransformerencoder_pb_kernel(tc, x, yt, ln1_g, ln1_b, Wq, bq, Wo, bo, out):
    nc = tc.nc
    x_view = x.flatten_outer_dims().rearrange("(p t) d -> p t d", t=TILES)
    yt_view = yt.flatten_outer_dims().rearrange("(p t) d -> p t d", t=TILES)
    out_view = out.flatten_outer_dims().rearrange("(p t) d -> p t d", t=TILES)

    with (
        tc.tile_pool(name="consts", bufs=1) as consts,
        tc.tile_pool(name="resident", bufs=1) as resident,
        tc.tile_pool(name="work", bufs=3) as work,
        tc.psum_pool(name="psum", bufs=2) as psum,
    ):
        x_sb = [resident.tile([P, CHUNK_TILES, D], BF16, name="x%d" % c) for c in range(CHUNKS)]
        yt_sb = [resident.tile([P, CHUNK_TILES, D], BF16, name="yt%d" % c) for c in range(CHUNKS)]
        wq_raw = consts.tile([P, PACK, D], BF16, name="wq_raw")
        wo_raw = consts.tile([P, PACK, D], BF16, name="wo_raw")
        vec_rows = consts.tile([P, P], BF16, name="vec_rows")
        bo_all = consts.tile([P, D], BF16, name="bo_all")

        def load_chunk(dst, view, c):
            nc.sync.dma_start(out=dst[c][:], in_=view[:, c * CHUNK_TILES : (c + 1) * CHUNK_TILES, :])

        def load_weight(dst, w):
            nc.sync.dma_start(out=dst[:], in_=w.rearrange("(j p) n -> p j n", p=P))

        load_chunk(x_sb, x_view, 0)
        nc.vector.memset(vec_rows[:], 0.0)
        for i, vec in enumerate((ln1_g, ln1_b, bq)):
            nc.sync.dma_start(
                out=vec_rows[i * PACK : (i + 1) * PACK, :], in_=vec.rearrange("(j c) -> j c", c=P)
            )
        load_weight(wq_raw, Wq)
        load_chunk(x_sb, x_view, 1)
        load_chunk(x_sb, x_view, 2)
        load_weight(wo_raw, Wo)
        for c in range(3, CHUNKS):
            load_chunk(x_sb, x_view, c)
            load_chunk(yt_sb, yt_view, c - 3)
        nc.sync.dma_start(out=bo_all[:], in_=bo.partition_broadcast(P))
        for c in range(CHUNKS - 3, CHUNKS):
            load_chunk(yt_sb, yt_view, c)

        warm = consts.tile([P, 1], F32, name="warm")
        nc.vector.memset(warm[:], 0.0)
        warm_out = consts.tile([P, 1], F32, name="warm_out")
        nc.scalar.activation(out=warm_out[:], in_=warm[:], func=ACT.Sigmoid)

        ident_bf16 = consts.tile([P, P], BF16, name="ident_bf16")
        make_identity(nc, ident_bf16[:])
        ident_f32 = consts.tile([P, P], F32, name="ident_f32")
        make_identity(nc, ident_f32[:])
        neg_half = consts.tile([P, CHUNK_TILES], F32, name="neg_half")
        nc.gpsimd.memset(neg_half[:], -0.5)

        wq_grouped = consts.tile([P, D, PACK], BF16, name="wq_grouped", align_bytes=64)
        wo_grouped = consts.tile([P, D, PACK], BF16, name="wo_grouped", align_bytes=64)
        wq_codes = consts.tile([P, D], U32, name="wq_codes", align_bytes=64)
        wq_scales = consts.tile([P, D], U8, name="wq_scales", align_bytes=64)
        wo_codes = consts.tile([P, D], U32, name="wo_codes", align_bytes=64)
        wo_scales = consts.tile([P, D], U8, name="wo_scales", align_bytes=64)
        cols = consts.tile([P, 3 * PACK], F32, name="cols")
        g_col = cols[:, 0:PACK]
        b_col = cols[:, PACK : 2 * PACK]
        bq_col = cols[:, 2 * PACK : 3 * PACK]

        rstd, shift, xn, xnT, hT, h_grouped, h_codes, h_scales = {}, {}, {}, {}, {}, {}, {}, {}
        qT, gate, ytT, y_grouped, y_codes, y_scales, o, res = {}, {}, {}, {}, {}, {}, {}, {}

        def regroup(copy, grouped, planes):
            copy(
                out=grouped[:].rearrange("p (c i) j -> p c j i", i=RUN),
                in_=planes[:].rearrange("p j (c i) -> p c j i", i=RUN),
            )

        def quantise(grouped, codes, scales):
            nc.vector.quantize_mx(
                out=codes[:].bitcast(FP8X4), scales=scales[:], in_=grouped[:].rearrange("p w j -> p (w j)")
            )

        def stats(c):
            bn = work.tile([P, CHUNK_TILES, 6], F32, name="bn")
            mean_var = work.tile([P, CHUNK_TILES, 2], F32, name="mean_var")
            for i in range(CHUNK_TILES):
                nc.vector.bn_stats(out=bn[:, i, :], in_=x_sb[c][:, i, :])
            for i in range(CHUNK_TILES):
                nc.vector.bn_aggr(out=mean_var[:, i, :], in_=bn[:, i, :])
            var_eps = work.tile([P, CHUNK_TILES], F32, name="var_eps")
            nc.gpsimd.tensor_scalar(
                out=var_eps[:], in0=mean_var[:, :, 1], scalar1=EPS, scalar2=None, op0=ALU.add
            )
            neg_mean = work.tile([P, CHUNK_TILES], F32, name="neg_mean")
            nc.gpsimd.tensor_scalar(
                out=neg_mean[:], in0=mean_var[:, :, 0], scalar1=-1.0, scalar2=None, op0=ALU.mult
            )
            rstd[c] = resident.tile([P, CHUNK_TILES], F32, name="rstd%d" % c)
            nc.gpsimd.tensor_tensor(out=rstd[c][:], in0=var_eps[:], in1=neg_half[:], op=ALU.pow)
            shift[c] = resident.tile([P, CHUNK_TILES], F32, name="shift%d" % c)
            nc.gpsimd.tensor_tensor(out=shift[c][:], in0=neg_mean[:], in1=rstd[c][:], op=ALU.mult)

        def normalise(c):
            xn[c] = work.tile([P, CHUNK_TILES, D], F32, name="xn")
            for i in range(CHUNK_TILES):
                nc.scalar.activation(
                    out=xn[c][:, i, :],
                    in_=x_sb[c][:, i, :],
                    func=ACT.Identity,
                    scale=rstd[c][:, i : i + 1],
                    bias=shift[c][:, i : i + 1],
                )

        def transpose_x(c):
            xnT[c] = []
            for b in range(2):
                bank = psum.tile([P, 2, CHUNK_ROWS], F32, name="xnT")
                for jj in range(2):
                    j = 2 * b + jj
                    for i in range(CHUNK_TILES):
                        nc.tensor.transpose(
                            bank[:, jj, i * P : (i + 1) * P], xn[c][:, i, j * P : (j + 1) * P], ident_f32[:]
                        )
                xnT[c].append(bank)

        def gain_shift(c):
            hT[c] = work.tile([P, PACK, CHUNK_ROWS], BF16, name="hT")
            for j in range(PACK):
                nc.scalar.activation(
                    out=hT[c][:, j, :],
                    in_=xnT[c][j // 2][:, j % 2, :],
                    func=ACT.Identity,
                    scale=g_col[:, j : j + 1],
                    bias=b_col[:, j : j + 1],
                )

        def group_h(c):
            h_grouped[c] = work.tile([P, CHUNK_ROWS, PACK], BF16, name="h_grouped", align_bytes=64)
            regroup(nc.vector.tensor_copy if c % 2 == 0 else nc.scalar.copy, h_grouped[c], hT[c])

        def quantise_h(c):
            h_codes[c] = work.tile([P, CHUNK_ROWS], U32, name="h_codes", align_bytes=64)
            h_scales[c] = work.tile([P, CHUNK_ROWS], U8, name="h_scales", align_bytes=64)
            quantise(h_grouped[c], h_codes[c], h_scales[c])

        def q_matmuls(c):
            qT[c] = []
            for b in range(2):
                bank = psum.tile([P, 2, CHUNK_ROWS], F32, name="qT")
                for jj in range(2):
                    j = 2 * b + jj
                    nc.tensor.matmul_mx(
                        out=bank[:, jj, :],
                        lhsT=wq_codes[:, j * P : (j + 1) * P].bitcast(FP8X4),
                        lhsT_scale=wq_scales[:, j * P : (j + 1) * P],
                        rhs=h_codes[c][:].bitcast(FP8X4),
                        rhs_scale=h_scales[c][:],
                        start=True,
                        stop=True,
                    )
                qT[c].append(bank)

        def sigmoid(c):
            gate[c] = work.tile([P, PACK, CHUNK_ROWS], F32, name="gate")
            for j in range(PACK):
                nc.scalar.activation(
                    out=gate[c][:, j, :],
                    in_=qT[c][j // 2][:, j % 2, :],
                    func=ACT.Sigmoid,
                    bias=bq_col[:, j : j + 1],
                )

        def transpose_yt(c):
            ytT[c] = psum.tile([P, PACK, CHUNK_ROWS], BF16, name="ytT")
            for j in range(PACK):
                for i in range(CHUNK_TILES):
                    nc.tensor.transpose(
                        ytT[c][:, j, i * P : (i + 1) * P], yt_sb[c][:, i, j * P : (j + 1) * P], ident_bf16[:]
                    )

        def product(c):
            y_grouped[c] = work.tile([P, CHUNK_ROWS, PACK], BF16, name="y_grouped", align_bytes=64)
            nc.vector.tensor_tensor(
                out=y_grouped[c][:],
                in0=ytT[c][:].rearrange("p j w -> p w j"),
                in1=gate[c][:].rearrange("p j w -> p w j"),
                op=ALU.mult,
            )

        def quantise_y(c):
            y_codes[c] = work.tile([P, CHUNK_ROWS], U32, name="y_codes", align_bytes=64)
            y_scales[c] = work.tile([P, CHUNK_ROWS], U8, name="y_scales", align_bytes=64)
            quantise(y_grouped[c], y_codes[c], y_scales[c])

        def out_matmuls(c):
            o[c] = []
            for i in range(CHUNK_TILES):
                bank = psum.tile([P, D], F32, name="o")
                nc.tensor.matmul_mx(
                    out=bank[:],
                    lhsT=y_codes[c][:, i * P : (i + 1) * P].bitcast(FP8X4),
                    lhsT_scale=y_scales[c][:, i * P : (i + 1) * P],
                    rhs=wo_codes[:].bitcast(FP8X4),
                    rhs_scale=wo_scales[:],
                    start=True,
                    stop=True,
                )
                o[c].append(bank)

        def residual(c):
            res[c] = resident.tile([P, CHUNK_TILES, D], F32, name="res%d" % c)
            nc.vector.tensor_tensor(
                out=res[c][:],
                in0=x_sb[c][:],
                in1=bo_all[:].unsqueeze(1).to_broadcast([P, CHUNK_TILES, D]),
                op=ALU.add,
            )

        def add_store(c, i):
            nc.vector.tensor_tensor(out=res[c][:, i, :], in0=o[c][i][:], in1=res[c][:, i, :], op=ALU.add)
            nc.sync.dma_start(out=out_view[:, c * CHUNK_TILES + i, :], in_=res[c][:, i, :])

        def add_first(c):
            add_store(c, 0)

        def add_second(c):
            add_store(c, 1)

        def run(stage, c):
            if 0 <= c < CHUNKS:
                stage(c)

        regroup(nc.scalar.copy, wq_grouped, wq_raw)
        for c in range(STATS_AHEAD):
            stats(c)
        cols_ps = psum.tile([P, P], BF16, name="cols_ps", tag="ytT")
        nc.tensor.transpose(cols_ps[:], vec_rows[:], ident_bf16[:])
        nc.scalar.copy(out=cols[:], in_=cols_ps[:, 0 : 3 * PACK])
        normalise(0)
        normalise(1)
        transpose_x(0)
        regroup(nc.vector.tensor_copy, wo_grouped, wo_raw)
        quantise(wq_grouped, wq_codes, wq_scales)
        quantise(wo_grouped, wo_codes, wo_scales)

        for s in range(CHUNKS + 2):
            run(gain_shift, s)
            run(group_h, s)
            run(sigmoid, s - 1)
            run(normalise, s + 2)
            run(transpose_x, s + 1)
            run(transpose_yt, s)
            run(add_first, s - 2)
            run(quantise_h, s)
            run(q_matmuls, s)
            run(product, s - 1)
            run(add_second, s - 2)
            run(quantise_y, s - 1)
            run(out_matmuls, s - 1)
            run(stats, s + STATS_AHEAD)
            run(residual, s)
